import numpy as np
import ml_dtypes


def mxq(x, axis, fmt="e4m3"):
    dtype, down = {"e4m3": (ml_dtypes.float8_e4m3fn, 7), "e5m2": (ml_dtypes.float8_e5m2, 14)}[fmt]
    v = np.moveaxis(np.asarray(x, np.float32).astype(ml_dtypes.bfloat16).astype(np.float64), axis, -1)
    blocks = v.reshape(v.shape[:-1] + (-1, 32))
    amax = np.abs(blocks).max(-1, keepdims=True)
    byte = np.maximum(np.where(amax > 0, np.frexp(amax)[1] - 1 + 127, 0) - down, 1)
    scale = np.exp2(byte - 127.0)
    codes = (blocks / scale).astype(np.float32).astype(dtype).astype(np.float64)
    return np.moveaxis((codes * scale).reshape(v.shape), -1, axis)


WIDE = False


def mx_kscale(k):
    if not WIDE:
        return np.ones(k)
    levels = np.array([10, -10, 5, -5, 0])
    a = np.random.permutation(np.resize(levels, k // 512 * 4)).reshape(k // 512, 4)
    idx = np.arange(k)
    return np.exp2(a[idx // 512, idx % 128 // 32])


BF16 = ml_dtypes.bfloat16


def bf(x):
    return np.asarray(x, np.float32).astype(BF16)


def f64(x):
    return np.asarray(x).astype(np.float64)


B, DIN, H1, H2, N, I, K, O = 4096, 2048, 1024, 512, 64, 16, 64, 16
NI = N * I
KO = K * O
SQ_EPS = 1e-8


def squash(t):
    sq = np.sum(t * t, axis=-1, keepdims=True)
    return (sq / (1.0 + sq)) * t / np.sqrt(sq + SQ_EPS)


def setup_inputs():
    s = mx_kscale(NI).reshape(N, I)
    return {"p": bf(np.random.standard_normal((B, N, I)) * s),
            "Wr": bf(np.random.standard_normal((N, K, O, I)) * K / np.sqrt(NI * O) / s[:, None, None, :])}


def reference(p, Wr):
    c = 1.0 / K
    pf = f64(p).reshape(B, NI)
    wf = f64(Wr).transpose(0, 3, 1, 2).reshape(NI, KO)
    s = (mxq(pf, 1, "e4m3") @ mxq(wf, 0, "e4m3")).reshape(B, K, O) * c
    return squash(s)

@@ -1,0 +1,233 @@
+from contextlib import ExitStack
+
+import concourse.mybir as mybir
+from concourse.masks import make_identity
+
+F32 = mybir.dt.float32
+BF16 = mybir.dt.bfloat16
+U32 = mybir.dt.uint32
+U8 = mybir.dt.uint8
+FP8X4 = mybir.dt.float8_e4m3fn_x4
+ACT = mybir.ActivationFunctionType
+ALU = mybir.AluOpType
+
+P = 128
+BATCH = 4096
+CAPS_IN = 64
+DIM_IN = 16
+CAPS_OUT = 64
+DIM_OUT = 16
+K = CAPS_IN * DIM_IN
+COLS = CAPS_OUT * DIM_OUT
+PACK = 4
+K_PASS = P * PACK
+PASSES = K // K_PASS
+CAPS_PASS = CAPS_IN // PASSES
+BANK = 512
+HALVES = COLS // BANK
+CAPS_BANK = BANK // DIM_OUT
+TILES = BATCH // P
+LOAD_TILES = 4
+COUPLING = 1.0 / CAPS_OUT
+SQ_EPS = 1e-8
+
+FLOPS = 2 * BATCH * K * COLS
+
+
+def tile_capsulenetwork_pb_t_kernel(tc, p, Wr, out):
+    nc = tc.nc
+    p_view = p.rearrange("(row t) n i -> row t (n i)", t=TILES)
+    out_view = out.rearrange("(row t) j o -> row t (j o)", t=TILES)
+    w_view = Wr.rearrange("n j (oh ol) i -> (j oh) n (ol i)", oh=2)
+
+    with ExitStack() as ctx:
+        const = ctx.enter_context(tc.tile_pool(name="const", bufs=1))
+        weights = ctx.enter_context(tc.tile_pool(name="weights", bufs=1))
+        rows = ctx.enter_context(tc.tile_pool(name="rows", bufs=1))
+        stage = ctx.enter_context(tc.tile_pool(name="stage", bufs=3))
+        packed = ctx.enter_context(tc.tile_pool(name="packed", bufs=4))
+        squash = ctx.enter_context(tc.tile_pool(name="squash", bufs=3))
+        result = ctx.enter_context(tc.tile_pool(name="result", bufs=4))
+        flip = ctx.enter_context(tc.psum_pool(name="flip", bufs=2))
+        sums = ctx.enter_context(tc.psum_pool(name="sums", bufs=6))
+        ctx.enter_context(tc.manual_schedule())
+
+        w_raw = weights.tile([P, CAPS_IN, 8 * DIM_IN], BF16)
+        for g in range(PASSES):
+            caps = slice(g * CAPS_PASS, (g + 1) * CAPS_PASS)
+            nc.sync.dma_start(out=w_raw[:, caps, :], in_=w_view[:, caps, :])
+        p_rows = []
+        for c in range(TILES // LOAD_TILES):
+            chunk = rows.tile([P, LOAD_TILES, K], BF16, name="p_rows%d" % c)
+            nc.sync.dma_start(out=chunk[:], in_=p_view[:, c * LOAD_TILES : (c + 1) * LOAD_TILES, :])
+            p_rows.append(chunk)
+
+        ident = const.tile([P, P], F32)
+        make_identity(nc, ident[:])
+        eps_bias = const.tile([P, 1], F32)
+        nc.vector.memset(eps_bias[:], SQ_EPS / (COUPLING * COUPLING))
+        table_warm = const.tile([P, 1], F32)
+        nc.scalar.activation(out=table_warm[:], in_=eps_bias[:], func=ACT.Sqrt)
+
+        w_raw_words = w_raw[:].bitcast(F32).rearrange("c n (ol w) -> c ol n w", ol=8)
+        w_sorted = weights.tile([P, PASSES, 8, K_PASS // 2], F32)
+        w_grouped = weights.tile([P, PASSES, COLS * PACK], BF16, align_bytes=64)
+        w_grouped_words = w_grouped[:].bitcast(F32).rearrange("r g (c ol u) -> r g c ol u", ol=8, u=2)
+        w_codes = weights.tile([P, PASSES, COLS], U32, align_bytes=64)
+        w_scales = weights.tile([P, PASSES, COLS], U8, align_bytes=64)
+        for g in range(PASSES):
+            caps = slice(g * CAPS_PASS, (g + 1) * CAPS_PASS)
+            for m in range(4):
+                nc.vector.tensor_copy(
+                    out=w_sorted[:, g, 2 * m : 2 * m + 2, :].rearrange("c ol (n w) -> c ol n w", w=8),
+                    in_=w_raw_words[:, 2 * m : 2 * m + 2, caps, :],
+                )
+            for m in range(4):
+                w_bank = sums.tile([P, 2, 2, P], F32, tag="bank")
+                for a in range(2):
+                    for u in range(2):
+                        nc.tensor.transpose(
+                            w_bank[:, a, u, :], w_sorted[:, g, 2 * m + a, u * P : (u + 1) * P], ident[:]
+                        )
+                copy = nc.scalar.copy if m < 2 else nc.vector.tensor_copy
+                copy(
+                    out=w_grouped_words[:, g, :, 2 * m : 2 * m + 2, :],
+                    in_=w_bank[:].rearrange("r a u c -> r c a u"),
+                )
+            nc.vector.quantize_mx(
+                out=w_codes[:, g, :].bitcast(FP8X4), scales=w_scales[:, g, :], in_=w_grouped[:, g, :]
+            )
+
+        flipped = {}
+        grouped = {}
+        codes = {}
+        scales = {}
+        banks = {}
+        squares = {}
+        norms = {}
+        factors = {}
+        squashed = {}
+
+        def transpose_rows(t):
+            words = p_rows[t // LOAD_TILES][:, t % LOAD_TILES, :].bitcast(F32)
+            flipped[t] = flip.tile([P, PASSES * 2, P], F32, name="flipped")
+            for x in range(PASSES * 2):
+                nc.tensor.transpose(flipped[t][:, x, :], words[:, x * P : (x + 1) * P], ident[:])
+
+        def group_rows(t):
+            if t % 2 == 0:
+                grouped[t // 2] = stage.tile([P, 2, PASSES, P * PACK], BF16, name="grouped", align_bytes=64)
+            dst = grouped[t // 2][:].bitcast(F32).rearrange("r e g (row u) -> r e g row u", u=2)
+            nc.scalar.copy(
+                out=dst[:, t % 2], in_=flipped[t][:].rearrange("r (g u) row -> r g row u", u=2)
+            )
+
+        def quantise_pair(pair):
+            codes[pair] = packed.tile([P, 2, PASSES, P], U32, name="codes", align_bytes=64)
+            scales[pair] = packed.tile([P, 2, PASSES, P], U8, name="scales", align_bytes=64)
+            nc.vector.quantize_mx(
+                out=codes[pair][:].rearrange("r e g row -> r (e g row)").bitcast(FP8X4),
+                scales=scales[pair][:].rearrange("r e g row -> r (e g row)"),
+                in_=grouped[pair][:].rearrange("r e g c -> r (e g c)"),
+            )
+
+        def multiply(t):
+            banks[t] = []
+            for h in range(HALVES):
+                cols = slice(h * BANK, (h + 1) * BANK)
+                bank = sums.tile([P, BANK], F32, tag="bank")
+                for g in range(PASSES):
+                    nc.tensor.matmul_mx(
+                        out=bank[:],
+                        lhsT=codes[t // 2][:, t % 2, g, :].bitcast(FP8X4),
+                        lhsT_scale=scales[t // 2][:, t % 2, g, :],
+                        rhs=w_codes[:, g, cols].bitcast(FP8X4),
+                        rhs_scale=w_scales[:, g, cols],
+                        start=(g == 0),
+                        stop=(g == PASSES - 1),
+                    )
+                banks[t].append(bank)
+
+        def square(t):
+            squares[t] = squash.tile([P, COLS], F32, name="squares")
+            for h in range(HALVES):
+                nc.scalar.activation(
+                    out=squares[t][:, h * BANK : (h + 1) * BANK], in_=banks[t][h][:], func=ACT.Square, scale=COUPLING
+                )
+
+        def norm(t):
+            q = squash.tile([P, CAPS_OUT], F32, name="q")
+            root = squash.tile([P, CAPS_OUT], F32, name="root")
+            nc.vector.tensor_reduce(
+                out=q[:],
+                in_=squares[t][:].rearrange("row (j o) -> row j o", o=DIM_OUT),
+                axis=mybir.AxisListType.X,
+                op=ALU.add,
+            )
+            nc.scalar.activation(
+                out=root[:], in_=q[:], func=ACT.Sqrt, bias=eps_bias[:], scale=1.0 / (COUPLING * COUPLING)
+            )
+            norms[t] = (q, root)
+
+        def denominator(t):
+            q, root = norms[t]
+            denom = squash.tile([P, CAPS_OUT], F32, name="denom")
+            nc.vector.scalar_tensor_tensor(
+                out=denom[:], in0=q[:], scalar=1.0, in1=root[:], op0=ALU.add, op1=ALU.mult
+            )
+            norms[t] = (q, denom)
+
+        def invert(t):
+            q, denom = norms[t]
+            inverse = squash.tile([P, CAPS_OUT], F32, name="inverse")
+            nc.vector.reciprocal(out=inverse[:], in_=denom[:])
+            norms[t] = (q, inverse)
+
+        def factor(t):
+            q, inverse = norms[t]
+            factors[t] = squash.tile([P, CAPS_OUT], F32, name="factor")
+            nc.vector.tensor_tensor(out=factors[t][:], in0=q[:], in1=inverse[:], op=ALU.mult)
+
+        def scale_half(t, h):
+            if h == 0:
+                squashed[t] = result.tile([P, COLS], F32, name="squashed")
+            nc.vector.tensor_tensor(
+                out=squashed[t][:, h * BANK : (h + 1) * BANK].rearrange("row (j o) -> row j o", o=DIM_OUT),
+                in0=banks[t][h][:].rearrange("row (j o) -> row j o", o=DIM_OUT),
+                in1=factors[t][:, h * CAPS_BANK : (h + 1) * CAPS_BANK]
+                .unsqueeze(2)
+                .to_broadcast([P, CAPS_BANK, DIM_OUT]),
+                op=ALU.mult,
+            )
+
+        def store(t):
+            nc.sync.dma_start(out=out_view[:, t, :], in_=squashed[t][:])
+
+        def live(t):
+            return 0 <= t < TILES
+
+        for s in range(-6, TILES + 1):
+            if live(s):
+                norm(s)
+            if live(s - 1):
+                scale_half(s - 1, 0)
+            if live(s):
+                denominator(s)
+            if live(s - 1):
+                scale_half(s - 1, 1)
+                store(s - 1)
+            if live(s):
+                invert(s)
+            if s % 2 == 0 and live(s + 4):
+                quantise_pair((s + 4) // 2)
+            if live(s):
+                factor(s)
+            if s % 2 == 0 and live(s + 6):
+                transpose_rows(s + 6)
+                transpose_rows(s + 7)
+            if live(s + 2):
+                multiply(s + 2)
+            if live(s + 6):
+                group_rows(s + 6)
+            if live(s + 2):
+                square(s + 2)

@@ -30,6 +30,7 @@ TILES = BATCH // P
 LOAD_TILES = 4
 COUPLING = 1.0 / CAPS_OUT
 SQ_EPS = 1e-8
+FOLDS = 2
 
 FLOPS = 2 * BATCH * K * COLS
 
@@ -48,8 +49,7 @@ def tile_capsulenetwork_pb_t_kernel(tc, p, Wr, out):
         packed = ctx.enter_context(tc.tile_pool(name="packed", bufs=4))
         squash = ctx.enter_context(tc.tile_pool(name="squash", bufs=3))
         result = ctx.enter_context(tc.tile_pool(name="result", bufs=4))
-        flip = ctx.enter_context(tc.psum_pool(name="flip", bufs=2))
-        sums = ctx.enter_context(tc.psum_pool(name="sums", bufs=6))
+        psum = ctx.enter_context(tc.psum_pool(name="psum", bufs=8))
         ctx.enter_context(tc.manual_schedule())
 
         w_raw = weights.tile([P, CAPS_IN, 8 * DIM_IN], BF16)
@@ -83,7 +83,7 @@ def tile_capsulenetwork_pb_t_kernel(tc, p, Wr, out):
                     in_=w_raw_words[:, 2 * m : 2 * m + 2, caps, :],
                 )
             for m in range(4):
-                w_bank = sums.tile([P, 2, 2, P], F32, tag="bank")
+                w_bank = psum.tile([P, 2, 2, P], F32, tag="bank")
                 for a in range(2):
                     for u in range(2):
                         nc.tensor.transpose(
@@ -107,10 +107,11 @@ def tile_capsulenetwork_pb_t_kernel(tc, p, Wr, out):
         norms = {}
         factors = {}
         squashed = {}
+        folded = {}
 
         def transpose_rows(t):
             words = p_rows[t // LOAD_TILES][:, t % LOAD_TILES, :].bitcast(F32)
-            flipped[t] = flip.tile([P, PASSES * 2, P], F32, name="flipped")
+            flipped[t] = psum.tile([P, PASSES * 2, P], F32, name="flipped", tag="bank")
             for x in range(PASSES * 2):
                 nc.tensor.transpose(flipped[t][:, x, :], words[:, x * P : (x + 1) * P], ident[:])
 
@@ -131,36 +132,50 @@ def tile_capsulenetwork_pb_t_kernel(tc, p, Wr, out):
                 in_=grouped[pair][:].rearrange("r e g c -> r (e g c)"),
             )
 
-        def multiply(t):
-            banks[t] = []
-            for h in range(HALVES):
-                cols = slice(h * BANK, (h + 1) * BANK)
-                bank = sums.tile([P, BANK], F32, tag="bank")
-                for g in range(PASSES):
-                    nc.tensor.matmul_mx(
-                        out=bank[:],
-                        lhsT=codes[t // 2][:, t % 2, g, :].bitcast(FP8X4),
-                        lhsT_scale=scales[t // 2][:, t % 2, g, :],
-                        rhs=w_codes[:, g, cols].bitcast(FP8X4),
-                        rhs_scale=w_scales[:, g, cols],
-                        start=(g == 0),
-                        stop=(g == PASSES - 1),
-                    )
-                banks[t].append(bank)
-
-        def square(t):
-            squares[t] = squash.tile([P, COLS], F32, name="squares")
-            for h in range(HALVES):
-                nc.scalar.activation(
-                    out=squares[t][:, h * BANK : (h + 1) * BANK], in_=banks[t][h][:], func=ACT.Square, scale=COUPLING
+        def multiply(t, h):
+            cols = slice(h * BANK, (h + 1) * BANK)
+            bank = psum.tile([P, BANK], F32, tag="bank")
+            for g in range(PASSES):
+                nc.tensor.matmul_mx(
+                    out=bank[:],
+                    lhsT=codes[t // 2][:, t % 2, g, :].bitcast(FP8X4),
+                    lhsT_scale=scales[t // 2][:, t % 2, g, :],
+                    rhs=w_codes[:, g, cols].bitcast(FP8X4),
+                    rhs_scale=w_scales[:, g, cols],
+                    start=(g == 0),
+                    stop=(g == PASSES - 1),
                 )
+            banks[t, h] = bank
+
+        def square(t, h):
+            if h == 0:
+                squares[t] = squash.tile([P, COLS], F32, name="squares")
+            nc.scalar.activation(
+                out=squares[t][:, h * BANK : (h + 1) * BANK], in_=banks[t, h][:], func=ACT.Square, scale=COUPLING
+            )
+
+        def fold(t):
+            src = squares[t]
+            width = DIM_OUT
+            for level in range(FOLDS):
+                width = width // 2
+                dst = squash.tile([P, CAPS_OUT * width], F32, name="folded%d" % level)
+                pairs = src[:].rearrange("row (j o) -> row j o", o=2 * width)
+                nc.gpsimd.tensor_tensor(
+                    out=dst[:].rearrange("row (j o) -> row j o", o=width),
+                    in0=pairs[:, :, 0:width],
+                    in1=pairs[:, :, width : 2 * width],
+                    op=ALU.add,
+                )
+                src = dst
+            folded[t] = src
 
         def norm(t):
             q = squash.tile([P, CAPS_OUT], F32, name="q")
             root = squash.tile([P, CAPS_OUT], F32, name="root")
             nc.vector.tensor_reduce(
                 out=q[:],
-                in_=squares[t][:].rearrange("row (j o) -> row j o", o=DIM_OUT),
+                in_=folded[t][:].rearrange("row (j o) -> row j o", j=CAPS_OUT),
                 axis=mybir.AxisListType.X,
                 op=ALU.add,
             )
@@ -193,7 +208,7 @@ def tile_capsulenetwork_pb_t_kernel(tc, p, Wr, out):
                 squashed[t] = result.tile([P, COLS], F32, name="squashed")
             nc.vector.tensor_tensor(
                 out=squashed[t][:, h * BANK : (h + 1) * BANK].rearrange("row (j o) -> row j o", o=DIM_OUT),
-                in0=banks[t][h][:].rearrange("row (j o) -> row j o", o=DIM_OUT),
+                in0=banks[t, h][:].rearrange("row (j o) -> row j o", o=DIM_OUT),
                 in1=factors[t][:, h * CAPS_BANK : (h + 1) * CAPS_BANK]
                 .unsqueeze(2)
                 .to_broadcast([P, CAPS_BANK, DIM_OUT]),
@@ -222,12 +237,15 @@ def tile_capsulenetwork_pb_t_kernel(tc, p, Wr, out):
                 quantise_pair((s + 4) // 2)
             if live(s):
                 factor(s)
-            if s % 2 == 0 and live(s + 6):
+            if live(s + 1):
+                fold(s + 1)
+            if live(s + 6):
                 transpose_rows(s + 6)
-                transpose_rows(s + 7)
             if live(s + 2):
-                multiply(s + 2)
+                multiply(s + 2, 0)
+                square(s + 2, 0)
             if live(s + 6):
                 group_rows(s + 6)
             if live(s + 2):
-                square(s + 2)
+                multiply(s + 2, 1)
+                square(s + 2, 1)

@@ -22,7 +22,10 @@ COLS = CAPS_OUT * DIM_OUT
 PACK = 4
 K_PASS = P * PACK
 PASSES = K // K_PASS
-CAPS_PASS = CAPS_IN // PASSES
+PLANES = 2
+CAPS_PLANE = CAPS_IN // (PASSES * PLANES)
+WORDS_IN = DIM_IN // 2
+COLS_PART = COLS // P
 BANK = 512
 HALVES = COLS // BANK
 CAPS_BANK = BANK // DIM_OUT
@@ -30,7 +33,11 @@ TILES = BATCH // P
 LOAD_TILES = 4
 COUPLING = 1.0 / CAPS_OUT
 SQ_EPS = 1e-8
-FOLDS = 2
+
+AHEAD_NORM = 1
+AHEAD_MULTIPLY = 3
+AHEAD_QUANTISE = 5
+AHEAD_TRANSPOSE = 7
 
 FLOPS = 2 * BATCH * K * COLS
 
@@ -39,22 +46,19 @@ def tile_capsulenetwork_pb_t_kernel(tc, p, Wr, out):
     nc = tc.nc
     p_view = p.rearrange("(row t) n i -> row t (n i)", t=TILES)
     out_view = out.rearrange("(row t) j o -> row t (j o)", t=TILES)
-    w_view = Wr.rearrange("n j (oh ol) i -> (j oh) n (ol i)", oh=2)
+    w_view = Wr.rearrange("n j (oh ol) i -> (j oh) n (ol i)", ol=COLS_PART)
 
     with ExitStack() as ctx:
         const = ctx.enter_context(tc.tile_pool(name="const", bufs=1))
         weights = ctx.enter_context(tc.tile_pool(name="weights", bufs=1))
         rows = ctx.enter_context(tc.tile_pool(name="rows", bufs=1))
-        stage = ctx.enter_context(tc.tile_pool(name="stage", bufs=3))
-        packed = ctx.enter_context(tc.tile_pool(name="packed", bufs=4))
-        squash = ctx.enter_context(tc.tile_pool(name="squash", bufs=3))
-        result = ctx.enter_context(tc.tile_pool(name="result", bufs=4))
+        work = ctx.enter_context(tc.tile_pool(name="work", bufs=4))
         psum = ctx.enter_context(tc.psum_pool(name="psum", bufs=8))
         ctx.enter_context(tc.manual_schedule())
 
-        w_raw = weights.tile([P, CAPS_IN, 8 * DIM_IN], BF16)
-        for g in range(PASSES):
-            caps = slice(g * CAPS_PASS, (g + 1) * CAPS_PASS)
+        w_raw = weights.tile([P, CAPS_IN, COLS_PART * DIM_IN], BF16)
+        for plane in range(PASSES * PLANES):
+            caps = slice(plane * CAPS_PLANE, (plane + 1) * CAPS_PLANE)
             nc.sync.dma_start(out=w_raw[:, caps, :], in_=w_view[:, caps, :])
         p_rows = []
         for c in range(TILES // LOAD_TILES):
@@ -69,34 +73,46 @@ def tile_capsulenetwork_pb_t_kernel(tc, p, Wr, out):
         table_warm = const.tile([P, 1], F32)
         nc.scalar.activation(out=table_warm[:], in_=eps_bias[:], func=ACT.Sqrt)
 
-        w_raw_words = w_raw[:].bitcast(F32).rearrange("c n (ol w) -> c ol n w", ol=8)
-        w_sorted = weights.tile([P, PASSES, 8, K_PASS // 2], F32)
+        w_raw_words = w_raw[:].bitcast(F32).rearrange("c n (ol w) -> c ol n w", ol=COLS_PART)
+        w_sorted = weights.tile([P, PASSES, COLS_PART, PLANES, P], F32)
         w_grouped = weights.tile([P, PASSES, COLS * PACK], BF16, align_bytes=64)
-        w_grouped_words = w_grouped[:].bitcast(F32).rearrange("r g (c ol u) -> r g c ol u", ol=8, u=2)
+        w_grouped_words = w_grouped[:].bitcast(F32).rearrange(
+            "r g (c ol u) -> r g c ol u", ol=COLS_PART, u=PLANES
+        )
         w_codes = weights.tile([P, PASSES, COLS], U32, align_bytes=64)
         w_scales = weights.tile([P, PASSES, COLS], U8, align_bytes=64)
-        for g in range(PASSES):
-            caps = slice(g * CAPS_PASS, (g + 1) * CAPS_PASS)
-            for m in range(4):
-                nc.vector.tensor_copy(
-                    out=w_sorted[:, g, 2 * m : 2 * m + 2, :].rearrange("c ol (n w) -> c ol n w", w=8),
-                    in_=w_raw_words[:, 2 * m : 2 * m + 2, caps, :],
-                )
-            for m in range(4):
-                w_bank = psum.tile([P, 2, 2, P], F32, tag="bank")
-                for a in range(2):
-                    for u in range(2):
-                        nc.tensor.transpose(
-                            w_bank[:, a, u, :], w_sorted[:, g, 2 * m + a, u * P : (u + 1) * P], ident[:]
-                        )
-                copy = nc.scalar.copy if m < 2 else nc.vector.tensor_copy
-                copy(
-                    out=w_grouped_words[:, g, :, 2 * m : 2 * m + 2, :],
-                    in_=w_bank[:].rearrange("r a u c -> r c a u"),
-                )
+        OL_BANK = 2
+
+        def quantise_weights(g):
             nc.vector.quantize_mx(
                 out=w_codes[:, g, :].bitcast(FP8X4), scales=w_scales[:, g, :], in_=w_grouped[:, g, :]
             )
+
+        for g in range(PASSES):
+            w_banks = []
+            for u in range(PLANES):
+                plane = g * PLANES + u
+                caps = slice(plane * CAPS_PLANE, (plane + 1) * CAPS_PLANE)
+                for m in range(COLS_PART // OL_BANK):
+                    ols = slice(m * OL_BANK, (m + 1) * OL_BANK)
+                    nc.vector.tensor_copy(
+                        out=w_sorted[:, g, ols, u, :].rearrange("c ol (n w) -> c ol n w", w=WORDS_IN),
+                        in_=w_raw_words[:, ols, caps, :],
+                    )
+                for m in range(COLS_PART // OL_BANK):
+                    if u == 0:
+                        w_banks.append(psum.tile([P, OL_BANK, PLANES, P], F32, name="w_bank", tag="bank"))
+                    for a in range(OL_BANK):
+                        nc.tensor.transpose(w_banks[m][:, a, u, :], w_sorted[:, g, m * OL_BANK + a, u, :], ident[:])
+            if g > 0:
+                quantise_weights(g - 1)
+            for m in range(COLS_PART // OL_BANK):
+                copy = nc.scalar.copy if m < 2 else nc.vector.tensor_copy
+                copy(
+                    out=w_grouped_words[:, g, :, m * OL_BANK : (m + 1) * OL_BANK, :],
+                    in_=w_banks[m][:].rearrange("r a u c -> r c a u"),
+                )
+        quantise_weights(PASSES - 1)
 
         flipped = {}
         grouped = {}
@@ -104,32 +120,34 @@ def tile_capsulenetwork_pb_t_kernel(tc, p, Wr, out):
         scales = {}
         banks = {}
         squares = {}
-        norms = {}
+        folded = {}
+        lengths = {}
+        roots = {}
+        denoms = {}
+        inverses = {}
         factors = {}
         squashed = {}
-        folded = {}
 
         def transpose_rows(t):
             words = p_rows[t // LOAD_TILES][:, t % LOAD_TILES, :].bitcast(F32)
-            flipped[t] = psum.tile([P, PASSES * 2, P], F32, name="flipped", tag="bank")
-            for x in range(PASSES * 2):
+            flipped[t] = psum.tile([P, PASSES * PLANES, P], F32, name="flipped", tag="bank")
+            for x in range(PASSES * PLANES):
                 nc.tensor.transpose(flipped[t][:, x, :], words[:, x * P : (x + 1) * P], ident[:])
 
         def group_rows(t):
-            if t % 2 == 0:
-                grouped[t // 2] = stage.tile([P, 2, PASSES, P * PACK], BF16, name="grouped", align_bytes=64)
-            dst = grouped[t // 2][:].bitcast(F32).rearrange("r e g (row u) -> r e g row u", u=2)
+            grouped[t] = work.tile([P, PASSES, P * PACK], BF16, name="grouped", align_bytes=64)
             nc.scalar.copy(
-                out=dst[:, t % 2], in_=flipped[t][:].rearrange("r (g u) row -> r g row u", u=2)
+                out=grouped[t][:].bitcast(F32).rearrange("r g (row u) -> r g row u", u=PLANES),
+                in_=flipped[t][:].rearrange("r (g u) row -> r g row u", u=PLANES),
             )
 
-        def quantise_pair(pair):
-            codes[pair] = packed.tile([P, 2, PASSES, P], U32, name="codes", align_bytes=64)
-            scales[pair] = packed.tile([P, 2, PASSES, P], U8, name="scales", align_bytes=64)
+        def quantise_rows(t):
+            codes[t] = work.tile([P, PASSES, P], U32, name="codes", align_bytes=64)
+            scales[t] = work.tile([P, PASSES, P], U8, name="scales", align_bytes=64)
             nc.vector.quantize_mx(
-                out=codes[pair][:].rearrange("r e g row -> r (e g row)").bitcast(FP8X4),
-                scales=scales[pair][:].rearrange("r e g row -> r (e g row)"),
-                in_=grouped[pair][:].rearrange("r e g c -> r (e g c)"),
+                out=codes[t][:].rearrange("r g row -> r (g row)").bitcast(FP8X4),
+                scales=scales[t][:].rearrange("r g row -> r (g row)"),
+                in_=grouped[t][:].rearrange("r g c -> r (g c)"),
             )
 
         def multiply(t, h):
@@ -138,8 +156,8 @@ def tile_capsulenetwork_pb_t_kernel(tc, p, Wr, out):
             for g in range(PASSES):
                 nc.tensor.matmul_mx(
                     out=bank[:],
-                    lhsT=codes[t // 2][:, t % 2, g, :].bitcast(FP8X4),
-                    lhsT_scale=scales[t // 2][:, t % 2, g, :],
+                    lhsT=codes[t][:, g, :].bitcast(FP8X4),
+                    lhsT_scale=scales[t][:, g, :],
                     rhs=w_codes[:, g, cols].bitcast(FP8X4),
                     rhs_scale=w_scales[:, g, cols],
                     start=(g == 0),
@@ -149,63 +167,53 @@ def tile_capsulenetwork_pb_t_kernel(tc, p, Wr, out):
 
         def square(t, h):
             if h == 0:
-                squares[t] = squash.tile([P, COLS], F32, name="squares")
+                squares[t] = work.tile([P, COLS], F32, name="squares")
+                folded[t] = work.tile([P, COLS // 2], F32, name="folded")
             nc.scalar.activation(
                 out=squares[t][:, h * BANK : (h + 1) * BANK], in_=banks[t, h][:], func=ACT.Square, scale=COUPLING
             )
+            pairs = squares[t][:, h * BANK : (h + 1) * BANK].rearrange("row (j o) -> row j o", o=DIM_OUT)
+            nc.gpsimd.tensor_tensor(
+                out=folded[t][:, h * BANK // 2 : (h + 1) * BANK // 2].rearrange("row (j o) -> row j o", o=DIM_OUT // 2),
+                in0=pairs[:, :, 0 : DIM_OUT // 2],
+                in1=pairs[:, :, DIM_OUT // 2 : DIM_OUT],
+                op=ALU.add,
+            )
 
-        def fold(t):
-            src = squares[t]
-            width = DIM_OUT
-            for level in range(FOLDS):
-                width = width // 2
-                dst = squash.tile([P, CAPS_OUT * width], F32, name="folded%d" % level)
-                pairs = src[:].rearrange("row (j o) -> row j o", o=2 * width)
-                nc.gpsimd.tensor_tensor(
-                    out=dst[:].rearrange("row (j o) -> row j o", o=width),
-                    in0=pairs[:, :, 0:width],
-                    in1=pairs[:, :, width : 2 * width],
-                    op=ALU.add,
-                )
-                src = dst
-            folded[t] = src
-
-        def norm(t):
-            q = squash.tile([P, CAPS_OUT], F32, name="q")
-            root = squash.tile([P, CAPS_OUT], F32, name="root")
+        def length(t):
+            lengths[t] = work.tile([P, CAPS_OUT], F32, name="lengths")
+            roots[t] = work.tile([P, CAPS_OUT], F32, name="roots")
             nc.vector.tensor_reduce(
-                out=q[:],
+                out=lengths[t][:],
                 in_=folded[t][:].rearrange("row (j o) -> row j o", j=CAPS_OUT),
                 axis=mybir.AxisListType.X,
                 op=ALU.add,
             )
             nc.scalar.activation(
-                out=root[:], in_=q[:], func=ACT.Sqrt, bias=eps_bias[:], scale=1.0 / (COUPLING * COUPLING)
+                out=roots[t][:],
+                in_=lengths[t][:],
+                func=ACT.Sqrt,
+                bias=eps_bias[:],
+                scale=1.0 / (COUPLING * COUPLING),
             )
-            norms[t] = (q, root)
 
         def denominator(t):
-            q, root = norms[t]
-            denom = squash.tile([P, CAPS_OUT], F32, name="denom")
+            denoms[t] = work.tile([P, CAPS_OUT], F32, name="denoms")
             nc.vector.scalar_tensor_tensor(
-                out=denom[:], in0=q[:], scalar=1.0, in1=root[:], op0=ALU.add, op1=ALU.mult
+                out=denoms[t][:], in0=lengths[t][:], scalar=1.0, in1=roots[t][:], op0=ALU.add, op1=ALU.mult
             )
-            norms[t] = (q, denom)
 
         def invert(t):
-            q, denom = norms[t]
-            inverse = squash.tile([P, CAPS_OUT], F32, name="inverse")
-            nc.vector.reciprocal(out=inverse[:], in_=denom[:])
-            norms[t] = (q, inverse)
+            inverses[t] = work.tile([P, CAPS_OUT], F32, name="inverses")
+            nc.vector.reciprocal(out=inverses[t][:], in_=denoms[t][:])
 
         def factor(t):
-            q, inverse = norms[t]
-            factors[t] = squash.tile([P, CAPS_OUT], F32, name="factor")
-            nc.vector.tensor_tensor(out=factors[t][:], in0=q[:], in1=inverse[:], op=ALU.mult)
+            factors[t] = work.tile([P, CAPS_OUT], F32, name="factors")
+            nc.vector.tensor_tensor(out=factors[t][:], in0=lengths[t][:], in1=inverses[t][:], op=ALU.mult)
 
         def scale_half(t, h):
             if h == 0:
-                squashed[t] = result.tile([P, COLS], F32, name="squashed")
+                squashed[t] = work.tile([P, COLS], F32, name="squashed")
             nc.vector.tensor_tensor(
                 out=squashed[t][:, h * BANK : (h + 1) * BANK].rearrange("row (j o) -> row j o", o=DIM_OUT),
                 in0=banks[t, h][:].rearrange("row (j o) -> row j o", o=DIM_OUT),
@@ -221,31 +229,29 @@ def tile_capsulenetwork_pb_t_kernel(tc, p, Wr, out):
         def live(t):
             return 0 <= t < TILES
 
-        for s in range(-6, TILES + 1):
-            if live(s):
-                norm(s)
-            if live(s - 1):
-                scale_half(s - 1, 0)
-            if live(s):
-                denominator(s)
-            if live(s - 1):
-                scale_half(s - 1, 1)
-                store(s - 1)
-            if live(s):
-                invert(s)
-            if s % 2 == 0 and live(s + 4):
-                quantise_pair((s + 4) // 2)
+        for s in range(-AHEAD_TRANSPOSE, TILES):
+            if live(s + AHEAD_NORM):
+                length(s + AHEAD_NORM)
             if live(s):
                 factor(s)
-            if live(s + 1):
-                fold(s + 1)
-            if live(s + 6):
-                transpose_rows(s + 6)
-            if live(s + 2):
-                multiply(s + 2, 0)
-                square(s + 2, 0)
-            if live(s + 6):
-                group_rows(s + 6)
-            if live(s + 2):
-                multiply(s + 2, 1)
-                square(s + 2, 1)
+            if live(s + AHEAD_QUANTISE):
+                quantise_rows(s + AHEAD_QUANTISE)
+            if live(s):
+                scale_half(s, 0)
+            if live(s + AHEAD_NORM):
+                denominator(s + AHEAD_NORM)
+            if live(s):
+                scale_half(s, 1)
+                store(s)
+            if live(s + AHEAD_NORM):
+                invert(s + AHEAD_NORM)
+            if live(s + AHEAD_TRANSPOSE):
+                transpose_rows(s + AHEAD_TRANSPOSE)
+            if live(s + AHEAD_MULTIPLY):
+                multiply(s + AHEAD_MULTIPLY, 0)
+                square(s + AHEAD_MULTIPLY, 0)
+            if live(s + AHEAD_TRANSPOSE):
+                group_rows(s + AHEAD_TRANSPOSE)
+            if live(s + AHEAD_MULTIPLY):
+                multiply(s + AHEAD_MULTIPLY, 1)
+                square(s + AHEAD_MULTIPLY, 1)

@@ -70,8 +70,10 @@ def tile_capsulenetwork_pb_t_kernel(tc, p, Wr, out):
         make_identity(nc, ident[:])
         eps_bias = const.tile([P, 1], F32)
         nc.vector.memset(eps_bias[:], SQ_EPS / (COUPLING * COUPLING))
+        one_bias = const.tile([P, 1], F32)
+        nc.vector.memset(one_bias[:], 1.0)
         table_warm = const.tile([P, 1], F32)
-        nc.scalar.activation(out=table_warm[:], in_=eps_bias[:], func=ACT.Sqrt)
+        nc.scalar.activation(out=table_warm[:], in_=one_bias[:], func=ACT.Abs_reciprocal_sqrt)
 
         w_raw_words = w_raw[:].bitcast(F32).rearrange("c n (ol w) -> c ol n w", ol=COLS_PART)
         w_sorted = weights.tile([P, PASSES, COLS_PART, PLANES, P], F32)
@@ -122,9 +124,9 @@ def tile_capsulenetwork_pb_t_kernel(tc, p, Wr, out):
         squares = {}
         folded = {}
         lengths = {}
-        roots = {}
-        denoms = {}
-        inverses = {}
+        inv_roots = {}
+        inv_1q = {}
+        units = {}
         factors = {}
         squashed = {}
 
@@ -182,34 +184,34 @@ def tile_capsulenetwork_pb_t_kernel(tc, p, Wr, out):
 
         def length(t):
             lengths[t] = work.tile([P, CAPS_OUT], F32, name="lengths")
-            roots[t] = work.tile([P, CAPS_OUT], F32, name="roots")
             nc.vector.tensor_reduce(
                 out=lengths[t][:],
                 in_=folded[t][:].rearrange("row (j o) -> row j o", j=CAPS_OUT),
                 axis=mybir.AxisListType.X,
                 op=ALU.add,
             )
+            inv_sqrt_1q = work.tile([P, CAPS_OUT], F32, name="inv_sqrt_1q")
+            inv_roots[t] = work.tile([P, CAPS_OUT], F32, name="inv_roots")
+            inv_1q[t] = work.tile([P, CAPS_OUT], F32, name="inv_1q")
             nc.scalar.activation(
-                out=roots[t][:],
+                out=inv_sqrt_1q[:], in_=lengths[t][:], func=ACT.Abs_reciprocal_sqrt, bias=one_bias[:]
+            )
+            nc.scalar.activation(
+                out=inv_roots[t][:],
                 in_=lengths[t][:],
-                func=ACT.Sqrt,
+                func=ACT.Abs_reciprocal_sqrt,
                 bias=eps_bias[:],
                 scale=1.0 / (COUPLING * COUPLING),
             )
+            nc.scalar.activation(out=inv_1q[t][:], in_=inv_sqrt_1q[:], func=ACT.Square)
 
-        def denominator(t):
-            denoms[t] = work.tile([P, CAPS_OUT], F32, name="denoms")
-            nc.vector.scalar_tensor_tensor(
-                out=denoms[t][:], in0=lengths[t][:], scalar=1.0, in1=roots[t][:], op0=ALU.add, op1=ALU.mult
-            )
-
-        def invert(t):
-            inverses[t] = work.tile([P, CAPS_OUT], F32, name="inverses")
-            nc.vector.reciprocal(out=inverses[t][:], in_=denoms[t][:])
+        def unit(t):
+            units[t] = work.tile([P, CAPS_OUT], F32, name="units")
+            nc.vector.tensor_tensor(out=units[t][:], in0=lengths[t][:], in1=inv_roots[t][:], op=ALU.mult)
 
         def factor(t):
             factors[t] = work.tile([P, CAPS_OUT], F32, name="factors")
-            nc.vector.tensor_tensor(out=factors[t][:], in0=lengths[t][:], in1=inverses[t][:], op=ALU.mult)
+            nc.vector.tensor_tensor(out=factors[t][:], in0=units[t][:], in1=inv_1q[t][:], op=ALU.mult)
 
         def scale_half(t, h):
             if h == 0:
@@ -232,19 +234,17 @@ def tile_capsulenetwork_pb_t_kernel(tc, p, Wr, out):
         for s in range(-AHEAD_TRANSPOSE, TILES):
             if live(s + AHEAD_NORM):
                 length(s + AHEAD_NORM)
-            if live(s):
-                factor(s)
             if live(s + AHEAD_QUANTISE):
                 quantise_rows(s + AHEAD_QUANTISE)
             if live(s):
                 scale_half(s, 0)
             if live(s + AHEAD_NORM):
-                denominator(s + AHEAD_NORM)
+                unit(s + AHEAD_NORM)
             if live(s):
                 scale_half(s, 1)
                 store(s)
             if live(s + AHEAD_NORM):
-                invert(s + AHEAD_NORM)
+                factor(s + AHEAD_NORM)
             if live(s + AHEAD_TRANSPOSE):
                 transpose_rows(s + AHEAD_TRANSPOSE)
             if live(s + AHEAD_MULTIPLY):

from contextlib import ExitStack

import concourse.mybir as mybir
from concourse.masks import make_identity

F32 = mybir.dt.float32
BF16 = mybir.dt.bfloat16
U32 = mybir.dt.uint32
U8 = mybir.dt.uint8
FP8X4 = mybir.dt.float8_e4m3fn_x4
ACT = mybir.ActivationFunctionType
ALU = mybir.AluOpType

P = 128
BATCH = 4096
CAPS_IN = 64
DIM_IN = 16
CAPS_OUT = 64
DIM_OUT = 16
K = CAPS_IN * DIM_IN
COLS = CAPS_OUT * DIM_OUT
PACK = 4
K_PASS = P * PACK
PASSES = K // K_PASS
PLANES = 2
CAPS_PLANE = CAPS_IN // (PASSES * PLANES)
WORDS_IN = DIM_IN // 2
COLS_PART = COLS // P
BANK = 512
HALVES = COLS // BANK
CAPS_BANK = BANK // DIM_OUT
TILES = BATCH // P
LOAD_TILES = 4
COUPLING = 1.0 / CAPS_OUT
SQ_EPS = 1e-8

AHEAD_NORM = 1
AHEAD_MULTIPLY = 3
AHEAD_QUANTISE = 5
AHEAD_TRANSPOSE = 7

FLOPS = 2 * BATCH * K * COLS


def tile_capsulenetwork_pb_t_kernel(tc, p, Wr, out):
    nc = tc.nc
    p_view = p.rearrange("(row t) n i -> row t (n i)", t=TILES)
    out_view = out.rearrange("(row t) j o -> row t (j o)", t=TILES)
    w_view = Wr.rearrange("n j (oh ol) i -> (j oh) n (ol i)", ol=COLS_PART)

    with ExitStack() as ctx:
        const = ctx.enter_context(tc.tile_pool(name="const", bufs=1))
        weights = ctx.enter_context(tc.tile_pool(name="weights", bufs=1))
        rows = ctx.enter_context(tc.tile_pool(name="rows", bufs=1))
        work = ctx.enter_context(tc.tile_pool(name="work", bufs=4))
        psum = ctx.enter_context(tc.psum_pool(name="psum", bufs=8))
        ctx.enter_context(tc.manual_schedule())

        w_raw = weights.tile([P, CAPS_IN, COLS_PART * DIM_IN], BF16)
        for plane in range(PASSES * PLANES):
            caps = slice(plane * CAPS_PLANE, (plane + 1) * CAPS_PLANE)
            nc.sync.dma_start(out=w_raw[:, caps, :], in_=w_view[:, caps, :])
        p_rows = []
        for c in range(TILES // LOAD_TILES):
            chunk = rows.tile([P, LOAD_TILES, K], BF16, name="p_rows%d" % c)
            nc.sync.dma_start(out=chunk[:], in_=p_view[:, c * LOAD_TILES : (c + 1) * LOAD_TILES, :])
            p_rows.append(chunk)

        ident = const.tile([P, P], F32)
        make_identity(nc, ident[:])
        eps_bias = const.tile([P, 1], F32)
        nc.vector.memset(eps_bias[:], SQ_EPS / (COUPLING * COUPLING))
        one_bias = const.tile([P, 1], F32)
        nc.vector.memset(one_bias[:], 1.0)
        table_warm = const.tile([P, 1], F32)
        nc.scalar.activation(out=table_warm[:], in_=one_bias[:], func=ACT.Abs_reciprocal_sqrt)

        w_raw_words = w_raw[:].bitcast(F32).rearrange("c n (ol w) -> c ol n w", ol=COLS_PART)
        w_sorted = weights.tile([P, PASSES, COLS_PART, PLANES, P], F32)
        w_grouped = weights.tile([P, PASSES, COLS * PACK], BF16, align_bytes=64)
        w_grouped_words = w_grouped[:].bitcast(F32).rearrange(
            "r g (c ol u) -> r g c ol u", ol=COLS_PART, u=PLANES
        )
        w_codes = weights.tile([P, PASSES, COLS], U32, align_bytes=64)
        w_scales = weights.tile([P, PASSES, COLS], U8, align_bytes=64)
        OL_BANK = 2

        def quantise_weights(g):
            nc.vector.quantize_mx(
                out=w_codes[:, g, :].bitcast(FP8X4), scales=w_scales[:, g, :], in_=w_grouped[:, g, :]
            )

        for g in range(PASSES):
            w_banks = []
            for u in range(PLANES):
                plane = g * PLANES + u
                caps = slice(plane * CAPS_PLANE, (plane + 1) * CAPS_PLANE)
                for m in range(COLS_PART // OL_BANK):
                    ols = slice(m * OL_BANK, (m + 1) * OL_BANK)
                    nc.vector.tensor_copy(
                        out=w_sorted[:, g, ols, u, :].rearrange("c ol (n w) -> c ol n w", w=WORDS_IN),
                        in_=w_raw_words[:, ols, caps, :],
                    )
                for m in range(COLS_PART // OL_BANK):
                    if u == 0:
                        w_banks.append(psum.tile([P, OL_BANK, PLANES, P], F32, name="w_bank", tag="bank"))
                    for a in range(OL_BANK):
                        nc.tensor.transpose(w_banks[m][:, a, u, :], w_sorted[:, g, m * OL_BANK + a, u, :], ident[:])
            if g > 0:
                quantise_weights(g - 1)
            for m in range(COLS_PART // OL_BANK):
                copy = nc.scalar.copy if m < 2 else nc.vector.tensor_copy
                copy(
                    out=w_grouped_words[:, g, :, m * OL_BANK : (m + 1) * OL_BANK, :],
                    in_=w_banks[m][:].rearrange("r a u c -> r c a u"),
                )
        quantise_weights(PASSES - 1)

        flipped = {}
        grouped = {}
        codes = {}
        scales = {}
        banks = {}
        squares = {}
        folded = {}
        lengths = {}
        inv_roots = {}
        inv_1q = {}
        units = {}
        factors = {}
        squashed = {}

        def transpose_rows(t):
            words = p_rows[t // LOAD_TILES][:, t % LOAD_TILES, :].bitcast(F32)
            flipped[t] = psum.tile([P, PASSES * PLANES, P], F32, name="flipped", tag="bank")
            for x in range(PASSES * PLANES):
                nc.tensor.transpose(flipped[t][:, x, :], words[:, x * P : (x + 1) * P], ident[:])

        def group_rows(t):
            grouped[t] = work.tile([P, PASSES, P * PACK], BF16, name="grouped", align_bytes=64)
            nc.scalar.copy(
                out=grouped[t][:].bitcast(F32).rearrange("r g (row u) -> r g row u", u=PLANES),
                in_=flipped[t][:].rearrange("r (g u) row -> r g row u", u=PLANES),
            )

        def quantise_rows(t):
            codes[t] = work.tile([P, PASSES, P], U32, name="codes", align_bytes=64)
            scales[t] = work.tile([P, PASSES, P], U8, name="scales", align_bytes=64)
            nc.vector.quantize_mx(
                out=codes[t][:].rearrange("r g row -> r (g row)").bitcast(FP8X4),
                scales=scales[t][:].rearrange("r g row -> r (g row)"),
                in_=grouped[t][:].rearrange("r g c -> r (g c)"),
            )

        def multiply(t, h):
            cols = slice(h * BANK, (h + 1) * BANK)
            bank = psum.tile([P, BANK], F32, tag="bank")
            for g in range(PASSES):
                nc.tensor.matmul_mx(
                    out=bank[:],
                    lhsT=codes[t][:, g, :].bitcast(FP8X4),
                    lhsT_scale=scales[t][:, g, :],
                    rhs=w_codes[:, g, cols].bitcast(FP8X4),
                    rhs_scale=w_scales[:, g, cols],
                    start=(g == 0),
                    stop=(g == PASSES - 1),
                )
            banks[t, h] = bank

        def square(t, h):
            if h == 0:
                squares[t] = work.tile([P, COLS], F32, name="squares")
                folded[t] = work.tile([P, COLS // 2], F32, name="folded")
            nc.scalar.activation(
                out=squares[t][:, h * BANK : (h + 1) * BANK], in_=banks[t, h][:], func=ACT.Square, scale=COUPLING
            )
            pairs = squares[t][:, h * BANK : (h + 1) * BANK].rearrange("row (j o) -> row j o", o=DIM_OUT)
            nc.gpsimd.tensor_tensor(
                out=folded[t][:, h * BANK // 2 : (h + 1) * BANK // 2].rearrange("row (j o) -> row j o", o=DIM_OUT // 2),
                in0=pairs[:, :, 0 : DIM_OUT // 2],
                in1=pairs[:, :, DIM_OUT // 2 : DIM_OUT],
                op=ALU.add,
            )

        def length(t):
            lengths[t] = work.tile([P, CAPS_OUT], F32, name="lengths")
            nc.vector.tensor_reduce(
                out=lengths[t][:],
                in_=folded[t][:].rearrange("row (j o) -> row j o", j=CAPS_OUT),
                axis=mybir.AxisListType.X,
                op=ALU.add,
            )
            inv_sqrt_1q = work.tile([P, CAPS_OUT], F32, name="inv_sqrt_1q")
            inv_roots[t] = work.tile([P, CAPS_OUT], F32, name="inv_roots")
            inv_1q[t] = work.tile([P, CAPS_OUT], F32, name="inv_1q")
            nc.scalar.activation(
                out=inv_sqrt_1q[:], in_=lengths[t][:], func=ACT.Abs_reciprocal_sqrt, bias=one_bias[:]
            )
            nc.scalar.activation(
                out=inv_roots[t][:],
                in_=lengths[t][:],
                func=ACT.Abs_reciprocal_sqrt,
                bias=eps_bias[:],
                scale=1.0 / (COUPLING * COUPLING),
            )
            nc.scalar.activation(out=inv_1q[t][:], in_=inv_sqrt_1q[:], func=ACT.Square)

        def unit(t):
            units[t] = work.tile([P, CAPS_OUT], F32, name="units")
            nc.vector.tensor_tensor(out=units[t][:], in0=lengths[t][:], in1=inv_roots[t][:], op=ALU.mult)

        def factor(t):
            factors[t] = work.tile([P, CAPS_OUT], F32, name="factors")
            nc.vector.tensor_tensor(out=factors[t][:], in0=units[t][:], in1=inv_1q[t][:], op=ALU.mult)

        def scale_half(t, h):
            if h == 0:
                squashed[t] = work.tile([P, COLS], F32, name="squashed")
            nc.vector.tensor_tensor(
                out=squashed[t][:, h * BANK : (h + 1) * BANK].rearrange("row (j o) -> row j o", o=DIM_OUT),
                in0=banks[t, h][:].rearrange("row (j o) -> row j o", o=DIM_OUT),
                in1=factors[t][:, h * CAPS_BANK : (h + 1) * CAPS_BANK]
                .unsqueeze(2)
                .to_broadcast([P, CAPS_BANK, DIM_OUT]),
                op=ALU.mult,
            )

        def store(t):
            nc.sync.dma_start(out=out_view[:, t, :], in_=squashed[t][:])

        def live(t):
            return 0 <= t < TILES

        for s in range(-AHEAD_TRANSPOSE, TILES):
            if live(s + AHEAD_NORM):
                length(s + AHEAD_NORM)
            if live(s + AHEAD_QUANTISE):
                quantise_rows(s + AHEAD_QUANTISE)
            if live(s):
                scale_half(s, 0)
            if live(s + AHEAD_NORM):
                unit(s + AHEAD_NORM)
            if live(s):
                scale_half(s, 1)
                store(s)
            if live(s + AHEAD_NORM):
                factor(s + AHEAD_NORM)
            if live(s + AHEAD_TRANSPOSE):
                transpose_rows(s + AHEAD_TRANSPOSE)
            if live(s + AHEAD_MULTIPLY):
                multiply(s + AHEAD_MULTIPLY, 0)
                square(s + AHEAD_MULTIPLY, 0)
            if live(s + AHEAD_TRANSPOSE):
                group_rows(s + AHEAD_TRANSPOSE)
            if live(s + AHEAD_MULTIPLY):
                multiply(s + AHEAD_MULTIPLY, 1)
                square(s + AHEAD_MULTIPLY, 1)
